import numpy as np
import ml_dtypes


def mxq(x, axis, fmt="e4m3"):
    dtype, down = {"e4m3": (ml_dtypes.float8_e4m3fn, 7), "e5m2": (ml_dtypes.float8_e5m2, 14)}[fmt]
    v = np.moveaxis(np.asarray(x, np.float32).astype(ml_dtypes.bfloat16).astype(np.float64), axis, -1)
    blocks = v.reshape(v.shape[:-1] + (-1, 32))
    amax = np.abs(blocks).max(-1, keepdims=True)
    byte = np.maximum(np.where(amax > 0, np.frexp(amax)[1] - 1 + 127, 0) - down, 1)
    scale = np.exp2(byte - 127.0)
    codes = (blocks / scale).astype(np.float32).astype(dtype).astype(np.float64)
    return np.moveaxis((codes * scale).reshape(v.shape), -1, axis)


WIDE = False


def mx_kscale(k):
    if not WIDE:
        return np.ones(k)
    levels = np.array([10, -10, 5, -5, 0])
    a = np.random.permutation(np.resize(levels, k // 512 * 4)).reshape(k // 512, 4)
    idx = np.arange(k)
    return np.exp2(a[idx // 512, idx % 128 // 32])


BF16 = ml_dtypes.bfloat16


def bf(x):
    return np.asarray(x, np.float32).astype(BF16)


def f64(x):
    return np.asarray(x).astype(np.float64)


WAY, SHOT, QUERY_SHOT, D, M = 8, 8, 8, 256, 512
G, Q = 4, 5
NS, NQ = WAY * SHOT, WAY * QUERY_SHOT


def log_softmax(v, axis):
    z = v - v.max(axis, keepdims=True)
    return z - np.log(np.exp(z).sum(axis, keepdims=True))


def setup_inputs():
    s = mx_kscale(M)
    return {"feature_map": bf(np.random.standard_normal((NS + NQ, D, M)) * np.sqrt(M) * s),
            "weight2": bf(np.random.uniform(0.0, 1.0, (NS, NQ, M)) / s),
            "scale": bf(G * Q * Q * SHOT / np.sqrt(D) * (1.0 + 0.1 * np.random.standard_normal(1)))}


def reference(feature_map, weight2, scale):
    fq = mxq(f64(feature_map), 2, "e4m3")
    wq = mxq(f64(weight2), 2, "e4m3")
    support = fq[:NS]
    query = fq[NS:]
    centroid = (wq @ support.transpose(0, 2, 1)) / M
    query_r = (wq.transpose(1, 0, 2) @ query.transpose(0, 2, 1)).transpose(1, 0, 2) / M
    l2 = ((centroid - query_r) ** 2).sum(-1)
    neg_l2 = -l2.T
    logits = neg_l2 / (G * Q * Q * SHOT) * f64(scale)
    return log_softmax(logits, 1)

@@ -1,0 +1,266 @@
+from contextlib import ExitStack
+
+import concourse.mybir as mybir
+from concourse.masks import make_identity
+
+F32 = mybir.dt.float32
+BF16 = mybir.dt.bfloat16
+U32 = mybir.dt.uint32
+U8 = mybir.dt.uint8
+FP8X4 = mybir.dt.float8_e4m3fn_x4
+ACT = mybir.ActivationFunctionType
+ALU = mybir.AluOpType
+AX = mybir.AxisListType
+
+P = 128
+NS = 64
+NQ = 64
+D = 256
+M = 512
+FLOPS = 2 * 2 * NS * NQ * D * M
+
+IMG = 4
+NSTEP = (NS + NQ) // IMG
+HALF = NS // IMG
+LOOKAHEAD = 4
+PIN = True
+
+
+def tile_proto_t_kernel(tc, feature_map, weight2, scale, out):
+    nc = tc.nc
+    with ExitStack() as ctx:
+        const = ctx.enter_context(tc.tile_pool(name="const", bufs=1))
+        xpool = ctx.enter_context(tc.tile_pool(name="xpool", bufs=LOOKAHEAD + 1))
+        wpool = ctx.enter_context(tc.tile_pool(name="wpool", bufs=LOOKAHEAD + 1))
+        work = ctx.enter_context(tc.tile_pool(name="work", bufs=3))
+        psum = ctx.enter_context(tc.psum_pool(name="psum", bufs=2))
+
+        ident = const.tile([P, P], F32)
+        make_identity(nc, ident[:])
+        sc_bf = const.tile([P, 1], BF16)
+        nc.scalar.dma_start(out=sc_bf[:], in_=scale.partition_broadcast(P))
+        a_sb = const.tile([P, 1], F32)
+        nc.vector.tensor_scalar_mul(a_sb[:], sc_bf[:], -1.0 / (800.0 * M * M))
+        l2col = const.tile([P, P], F32)
+        nc.vector.memset(l2col[:], 0.0)
+        warm = const.tile([P, 1], F32)
+        nc.scalar.activation(out=warm[:], in_=l2col[:, 0:1], func=ACT.Exp)
+
+        csb = const.tile([P, 2 * NQ * NS], F32)
+        csb4 = csb[:].rearrange("p (j q s) -> p j q s", j=2, q=NQ, s=NS)
+        gb = const.tile([P, NQ * NS * 4], BF16, align_bytes=64)
+        gb4 = gb[:].bitcast(F32).rearrange("p (q s u) -> p q s u", q=NQ, s=NS, u=2)
+        wbc = const.tile([P, NQ * NS], U32, align_bytes=64)
+        wbs = const.tile([P, NQ * NS], U8, align_bytes=64)
+
+        wrows = weight2.rearrange("s q m -> (s q) m").rearrange("(t p) m -> p t m", p=P)
+
+        xs = {}
+        ws = {}
+        xt = {}
+        wt = {}
+        gx = {}
+        ga = {}
+        xc = {}
+        xsc = {}
+        wac = {}
+        was = {}
+        mm = {}
+        diff = {}
+        dt = {}
+
+        def load(g):
+            if g >= NSTEP:
+                return
+            xs[g] = xpool.tile([P, IMG * 1024], BF16, name="xs", tag="xs")
+            dst = xs[g][:].rearrange("p (i f) -> p i f", i=IMG)
+            src = feature_map[IMG * g : IMG * (g + 1)].rearrange("i (p j) m -> p i (j m)", j=2)
+            if g == 0 or g == NSTEP - 1:
+                for i in range(IMG):
+                    nc.sync.dma_start(out=dst[:, i, :], in_=src[:, i, :])
+            else:
+                nc.sync.dma_start(out=dst, in_=src)
+            if g < HALF:
+                ws[g] = wpool.tile([P, 2 * M], BF16, name="ws", tag="ws")
+                nc.sync.dma_start(
+                    out=ws[g][:].rearrange("p (t m) -> p t m", t=2), in_=wrows[:, 2 * g : 2 * g + 2, :]
+                )
+
+        def transp(g):
+            if g >= NSTEP:
+                return
+            if g < HALF:
+                wt[g] = psum.tile([P, 2, 256], F32, name="wt", tag="aux", bufs=2)
+                ww = ws[g][:].bitcast(F32)
+                for t in range(2):
+                    for u in range(2):
+                        nc.tensor.transpose(
+                            wt[g][:, u, t * P : (t + 1) * P], ww[:, t * 256 + u * P : t * 256 + (u + 1) * P], ident[:]
+                        )
+            xw = xs[g][:].bitcast(F32)
+            for i in range(IMG):
+                xt[g, i] = psum.tile([P, 2, 256], F32, name="xt", tag="xt", bufs=4)
+                for j in range(2):
+                    for u in range(2):
+                        c0 = i * 512 + j * 256 + u * P
+                        nc.tensor.transpose(xt[g, i][:, u, j * P : (j + 1) * P], xw[:, c0 : c0 + P], ident[:])
+
+        def copy_x(g, i, on_vector):
+            dst = gx[g][:].bitcast(F32)[:, i * 512 : (i + 1) * 512].rearrange("p (c u) -> p c u", u=2)
+            src = xt[g, i][:].rearrange("p u c -> p c u")
+            if on_vector:
+                nc.vector.tensor_copy(out=dst, in_=src)
+            else:
+                nc.scalar.copy(out=dst, in_=src)
+
+        def copies(g):
+            if g >= NSTEP:
+                return
+            gx[g] = work.tile([P, IMG * 1024], BF16, name="gx", tag="gx", align_bytes=64)
+            if g < HALF:
+                ga[g] = work.tile([P, 1024], BF16, name="ga", tag="ga", align_bytes=64)
+                nc.vector.tensor_copy(
+                    out=ga[g][:].bitcast(F32).rearrange("p (c u) -> p c u", u=2),
+                    in_=wt[g][:].rearrange("p u c -> p c u"),
+                )
+                nc.vector.tensor_copy(
+                    out=gb4[:, :, IMG * g : IMG * (g + 1), :],
+                    in_=wt[g][:].rearrange("p u (s q) -> p q s u", s=IMG, q=NQ),
+                )
+                for i in range(IMG):
+                    copy_x(g, i, False)
+            else:
+                for i in range(IMG):
+                    copy_x(g, i, i == IMG - 1)
+
+        def quant_wa(g):
+            if g >= HALF:
+                return
+            wac[g] = work.tile([P, 256], U32, name="wac", tag="wac", align_bytes=64)
+            was[g] = work.tile([P, 256], U8, name="was", tag="was", align_bytes=64)
+            nc.vector.quantize_mx(out=wac[g][:].bitcast(FP8X4), scales=was[g][:], in_=ga[g][:])
+
+        def quant_wb(k):
+            nc.vector.quantize_mx(
+                out=wbc[:, k * 1024 : (k + 1) * 1024].bitcast(FP8X4),
+                scales=wbs[:, k * 1024 : (k + 1) * 1024],
+                in_=gb[:, k * 4096 : (k + 1) * 4096],
+            )
+
+        def quant_x(g):
+            if g < 0 or g >= NSTEP:
+                return
+            xc[g] = work.tile([P, IMG * 256], U32, name="xc", tag="xc", align_bytes=64)
+            xsc[g] = work.tile([P, IMG * 256], U8, name="xsc", tag="xsc", align_bytes=64)
+            nc.vector.quantize_mx(out=xc[g][:].bitcast(FP8X4), scales=xsc[g][:], in_=gx[g][:])
+
+        def mx(g):
+            if g < 0 or g >= NSTEP:
+                return
+            mm[g] = psum.tile([P, 512], F32, name="mm", tag="mm", bufs=2)
+            for i in range(IMG):
+                for j in range(2):
+                    c0 = i * 256 + j * P
+                    if g < HALF:
+                        slot = j * IMG + i
+                        rhs = wac[g][:, i * 64 : (i + 1) * 64]
+                        rhs_s = was[g][:, i * 64 : (i + 1) * 64]
+                    else:
+                        slot = (i // 2) * 4 + j * 2 + (i % 2)
+                        q = IMG * (g - HALF) + i
+                        rhs = wbc[:, q * 64 : (q + 1) * 64]
+                        rhs_s = wbs[:, q * 64 : (q + 1) * 64]
+                    nc.tensor.matmul_mx(
+                        out=mm[g][:, slot * 64 : (slot + 1) * 64],
+                        lhsT=xc[g][:, c0 : c0 + P].bitcast(FP8X4),
+                        lhsT_scale=xsc[g][:, c0 : c0 + P],
+                        rhs=rhs.bitcast(FP8X4),
+                        rhs_scale=rhs_s,
+                        start=True,
+                        stop=True,
+                    )
+
+        def ccopy(g):
+            if g < 0 or g >= HALF:
+                return
+            nc.scalar.copy(
+                out=csb4[:, :, :, IMG * g : IMG * (g + 1)],
+                in_=mm[g][:].rearrange("p (j i q) -> p j q i", j=2, i=IMG, q=NQ),
+            )
+
+        def sub(g):
+            if g < HALF or g >= NSTEP:
+                return
+            h = g - HALF
+            diff[g] = work.tile([P, 512], F32, name="diff", tag="diff")
+            nc.vector.tensor_tensor(
+                out=diff[g][:].rearrange("p (a j f) -> p a j f", a=2, j=2),
+                in0=mm[g][:].rearrange("p (a j f) -> p a j f", a=2, j=2),
+                in1=csb4[:, :, IMG * h : IMG * (h + 1), :].rearrange("p j (a b) s -> p a j (b s)", a=2, b=2),
+                op=ALU.subtract,
+            )
+
+        def dtr(g):
+            if g < HALF or g >= NSTEP:
+                return
+            dt[g] = psum.tile([P, 512], F32, name="dt", tag="aux", bufs=2)
+            for b in range(4):
+                nc.tensor.transpose(dt[g][:, b * P : (b + 1) * P], diff[g][:, b * P : (b + 1) * P], ident[:])
+
+        def sq(g):
+            if g < HALF or g >= NSTEP:
+                return
+            h = g - HALF
+            for a in range(2):
+                junk = work.tile([P, 256], F32, name="junk", tag="junk")
+                nc.scalar.activation(
+                    out=junk[:],
+                    in_=dt[g][:, a * 256 : (a + 1) * 256],
+                    func=ACT.Square,
+                    accum_out=l2col[:, 2 * h + a : 2 * h + a + 1],
+                )
+
+        if PIN:
+            ctx.enter_context(tc.manual_schedule())
+
+        for g in range(LOOKAHEAD):
+            load(g)
+        for k in range(NSTEP + 3):
+            load(k + LOOKAHEAD)
+            quant_x(k - 1)
+            if k >= HALF and (k - HALF) % 4 == 3 and k < HALF + 12:
+                quant_wb((k - HALF) // 4 + 1)
+            sub(k - 2)
+            ccopy(k - 2)
+            dtr(k - 3)
+            sq(k - 3)
+            transp(k)
+            copies(k)
+            quant_wa(k)
+            if k == HALF - 1:
+                quant_wb(0)
+            mx(k - 1)
+
+        l2t = psum.tile([P, P], F32, name="l2t", tag="aux", bufs=2)
+        nc.tensor.transpose(l2t[:], l2col[:], ident[:])
+        lg = const.tile([P, 2, NS], F32)
+        nc.vector.tensor_scalar_mul(lg[:].rearrange("p a s -> p (a s)"), l2t[:], a_sb[:, 0:1])
+        top = const.tile([P, 2], F32)
+        nc.vector.tensor_reduce(out=top[:], in_=lg[:], axis=AX.X, op=ALU.max)
+        z = const.tile([P, 2, NS], F32)
+        nc.vector.tensor_tensor(
+            out=z[:], in0=lg[:], in1=top[:].unsqueeze(2).to_broadcast([P, 2, NS]), op=ALU.subtract
+        )
+        ez = const.tile([P, 2, NS], F32)
+        tot = const.tile([P, 2], F32)
+        for a in range(2):
+            nc.scalar.activation(out=ez[:, a, :], in_=z[:, a, :], func=ACT.Exp, accum_out=tot[:, a : a + 1])
+        ltot = const.tile([P, 2], F32)
+        nc.scalar.activation(out=ltot[:], in_=tot[:], func=ACT.Ln)
+        res = const.tile([P, 2, NS], F32)
+        nc.vector.tensor_tensor(
+            out=res[:], in0=z[:], in1=ltot[:].unsqueeze(2).to_broadcast([P, 2, NS]), op=ALU.subtract
+        )
+        nc.sync.dma_start(
+            out=out.rearrange("(u a) s -> u (a s)", a=2), in_=res[0:32].rearrange("p a s -> p (a s)")
+        )

@@ -7,6 +7,7 @@ F32 = mybir.dt.float32
 BF16 = mybir.dt.bfloat16
 U32 = mybir.dt.uint32
 U8 = mybir.dt.uint8
+I32 = mybir.dt.int32
 FP8X4 = mybir.dt.float8_e4m3fn_x4
 ACT = mybir.ActivationFunctionType
 ALU = mybir.AluOpType
@@ -24,6 +25,7 @@ NSTEP = (NS + NQ) // IMG
 HALF = NS // IMG
 LOOKAHEAD = 4
 PIN = True
+WIDTHS = (128, 128, 128, 128, 128, 128, 128, 64)
 
 
 def tile_proto_t_kernel(tc, feature_map, weight2, scale, out):
@@ -50,8 +52,12 @@ def tile_proto_t_kernel(tc, feature_map, weight2, scale, out):
         csb4 = csb[:].rearrange("p (j q s) -> p j q s", j=2, q=NQ, s=NS)
         gb = const.tile([P, NQ * NS * 4], BF16, align_bytes=64)
         gb4 = gb[:].bitcast(F32).rearrange("p (q s u) -> p q s u", q=NQ, s=NS, u=2)
-        wbc = const.tile([P, NQ * NS], U32, align_bytes=64)
-        wbs = const.tile([P, NQ * NS], U8, align_bytes=64)
+        wbc = const.tile([P, NQ * NS + 64], U32, align_bytes=64)
+        wbs = const.tile([P, NQ * NS + 64], U8, align_bytes=64)
+        wac = const.tile([P, NQ * NS + 64], U32, align_bytes=64)
+        was = const.tile([P, NQ * NS + 64], U8, align_bytes=64)
+        for pad in (wbc, wbs, wac, was):
+            nc.vector.memset(pad[:, NQ * NS : NQ * NS + 64].bitcast(I32), 0)
 
         wrows = weight2.rearrange("s q m -> (s q) m").rearrange("(t p) m -> p t m", p=P)
 
@@ -63,8 +69,6 @@ def tile_proto_t_kernel(tc, feature_map, weight2, scale, out):
         ga = {}
         xc = {}
         xsc = {}
-        wac = {}
-        was = {}
         mm = {}
         diff = {}
         dt = {}
@@ -136,9 +140,9 @@ def tile_proto_t_kernel(tc, feature_map, weight2, scale, out):
         def quant_wa(g):
             if g >= HALF:
                 return
-            wac[g] = work.tile([P, 256], U32, name="wac", tag="wac", align_bytes=64)
-            was[g] = work.tile([P, 256], U8, name="was", tag="was", align_bytes=64)
-            nc.vector.quantize_mx(out=wac[g][:].bitcast(FP8X4), scales=was[g][:], in_=ga[g][:])
+            nc.vector.quantize_mx(
+                out=wac[:, 256 * g : 256 * (g + 1)].bitcast(FP8X4), scales=was[:, 256 * g : 256 * (g + 1)], in_=ga[g][:]
+            )
 
         def quant_wb(k):
             nc.vector.quantize_mx(
@@ -158,27 +162,25 @@ def tile_proto_t_kernel(tc, feature_map, weight2, scale, out):
             if g < 0 or g >= NSTEP:
                 return
             mm[g] = psum.tile([P, 512], F32, name="mm", tag="mm", bufs=2)
-            for i in range(IMG):
-                for j in range(2):
-                    c0 = i * 256 + j * P
-                    if g < HALF:
-                        slot = j * IMG + i
-                        rhs = wac[g][:, i * 64 : (i + 1) * 64]
-                        rhs_s = was[g][:, i * 64 : (i + 1) * 64]
-                    else:
-                        slot = (i // 2) * 4 + j * 2 + (i % 2)
-                        q = IMG * (g - HALF) + i
-                        rhs = wbc[:, q * 64 : (q + 1) * 64]
-                        rhs_s = wbs[:, q * 64 : (q + 1) * 64]
-                    nc.tensor.matmul_mx(
-                        out=mm[g][:, slot * 64 : (slot + 1) * 64],
-                        lhsT=xc[g][:, c0 : c0 + P].bitcast(FP8X4),
-                        lhsT_scale=xsc[g][:, c0 : c0 + P],
-                        rhs=rhs.bitcast(FP8X4),
-                        rhs_scale=rhs_s,
-                        start=True,
-                        stop=True,
-                    )
+            for slot in range(8):
+                if g < HALF:
+                    j, i = slot // IMG, slot % IMG
+                    codes, planes = wac, was
+                else:
+                    i, j = (slot // 4) * 2 + slot % 2, (slot // 2) % 2
+                    codes, planes = wbc, wbs
+                c0 = i * 256 + j * P
+                w0 = (IMG * (g % HALF) + i) * 64
+                n = WIDTHS[slot]
+                nc.tensor.matmul_mx(
+                    out=mm[g][:, slot * 64 : slot * 64 + n],
+                    lhsT=xc[g][:, c0 : c0 + P].bitcast(FP8X4),
+                    lhsT_scale=xsc[g][:, c0 : c0 + P],
+                    rhs=codes[:, w0 : w0 + n].bitcast(FP8X4),
+                    rhs_scale=planes[:, w0 : w0 + n],
+                    start=True,
+                    stop=True,
+                )
 
         def ccopy(g):
             if g < 0 or g >= HALF:

@@ -80,34 +80,38 @@ def tile_proto_t_kernel(tc, feature_map, weight2, scale, out):
             dst = xs[g][:].rearrange("p (i f) -> p i f", i=IMG)
             src = feature_map[IMG * g : IMG * (g + 1)].rearrange("i (p j) m -> p i (j m)", j=2)
             if g == 0 or g == NSTEP - 1:
-                for i in range(IMG):
-                    nc.sync.dma_start(out=dst[:, i, :], in_=src[:, i, :])
-            else:
-                nc.sync.dma_start(out=dst, in_=src)
+                nc.sync.dma_start(out=dst[:, 0, :], in_=src[:, 0, :])
             if g < HALF:
                 ws[g] = wpool.tile([P, 2 * M], BF16, name="ws", tag="ws")
                 nc.sync.dma_start(
                     out=ws[g][:].rearrange("p (t m) -> p t m", t=2), in_=wrows[:, 2 * g : 2 * g + 2, :]
                 )
+            if g == 0 or g == NSTEP - 1:
+                for i in range(1, IMG):
+                    nc.sync.dma_start(out=dst[:, i, :], in_=src[:, i, :])
+            else:
+                nc.sync.dma_start(out=dst, in_=src)
 
-        def transp(g):
+        def transp_w(g):
+            if g >= HALF:
+                return
+            wt[g] = psum.tile([P, 2, 256], F32, name="wt", tag="aux", bufs=2)
+            ww = ws[g][:].bitcast(F32)
+            for t in range(2):
+                for u in range(2):
+                    nc.tensor.transpose(
+                        wt[g][:, u, t * P : (t + 1) * P], ww[:, t * 256 + u * P : t * 256 + (u + 1) * P], ident[:]
+                    )
+
+        def transp_x(g, i):
             if g >= NSTEP:
                 return
-            if g < HALF:
-                wt[g] = psum.tile([P, 2, 256], F32, name="wt", tag="aux", bufs=2)
-                ww = ws[g][:].bitcast(F32)
-                for t in range(2):
-                    for u in range(2):
-                        nc.tensor.transpose(
-                            wt[g][:, u, t * P : (t + 1) * P], ww[:, t * 256 + u * P : t * 256 + (u + 1) * P], ident[:]
-                        )
             xw = xs[g][:].bitcast(F32)
-            for i in range(IMG):
-                xt[g, i] = psum.tile([P, 2, 256], F32, name="xt", tag="xt", bufs=4)
-                for j in range(2):
-                    for u in range(2):
-                        c0 = i * 512 + j * 256 + u * P
-                        nc.tensor.transpose(xt[g, i][:, u, j * P : (j + 1) * P], xw[:, c0 : c0 + P], ident[:])
+            xt[g, i] = psum.tile([P, 2, 256], F32, name="xt", tag="xt", bufs=4)
+            for j in range(2):
+                for u in range(2):
+                    c0 = i * 512 + j * 256 + u * P
+                    nc.tensor.transpose(xt[g, i][:, u, j * P : (j + 1) * P], xw[:, c0 : c0 + P], ident[:])
 
         def copy_x(g, i, on_vector):
             dst = gx[g][:].bitcast(F32)[:, i * 512 : (i + 1) * 512].rearrange("p (c u) -> p c u", u=2)
@@ -117,28 +121,31 @@ def tile_proto_t_kernel(tc, feature_map, weight2, scale, out):
             else:
                 nc.scalar.copy(out=dst, in_=src)
 
-        def copies(g):
+        def copies_w(g):
+            if g < 0 or g >= HALF:
+                return
+            ga[g] = work.tile([P, 1024], BF16, name="ga", tag="ga", align_bytes=64)
+            nc.vector.tensor_copy(
+                out=ga[g][:].bitcast(F32).rearrange("p (c u) -> p c u", u=2),
+                in_=wt[g][:].rearrange("p u c -> p c u"),
+            )
+            nc.vector.tensor_copy(
+                out=gb4[:, :, IMG * g : IMG * (g + 1), :],
+                in_=wt[g][:].rearrange("p u (s q) -> p q s u", s=IMG, q=NQ),
+            )
+
+        def copies_x(g):
             if g >= NSTEP:
                 return
             gx[g] = work.tile([P, IMG * 1024], BF16, name="gx", tag="gx", align_bytes=64)
-            if g < HALF:
-                ga[g] = work.tile([P, 1024], BF16, name="ga", tag="ga", align_bytes=64)
-                nc.vector.tensor_copy(
-                    out=ga[g][:].bitcast(F32).rearrange("p (c u) -> p c u", u=2),
-                    in_=wt[g][:].rearrange("p u c -> p c u"),
-                )
-                nc.vector.tensor_copy(
-                    out=gb4[:, :, IMG * g : IMG * (g + 1), :],
-                    in_=wt[g][:].rearrange("p u (s q) -> p q s u", s=IMG, q=NQ),
-                )
-                for i in range(IMG):
-                    copy_x(g, i, False)
-            else:
-                for i in range(IMG):
-                    copy_x(g, i, i == IMG - 1)
+            for i in range(IMG):
+                if g == NSTEP - 1:
+                    copy_x(g, i, i % 2 == 1)
+                else:
+                    copy_x(g, i, g >= HALF and i == IMG - 1)
 
         def quant_wa(g):
-            if g >= HALF:
+            if g < 0 or g >= HALF:
                 return
             nc.vector.quantize_mx(
                 out=wac[:, 256 * g : 256 * (g + 1)].bitcast(FP8X4), scales=was[:, 256 * g : 256 * (g + 1)], in_=ga[g][:]
@@ -156,7 +163,14 @@ def tile_proto_t_kernel(tc, feature_map, weight2, scale, out):
                 return
             xc[g] = work.tile([P, IMG * 256], U32, name="xc", tag="xc", align_bytes=64)
             xsc[g] = work.tile([P, IMG * 256], U8, name="xsc", tag="xsc", align_bytes=64)
-            nc.vector.quantize_mx(out=xc[g][:].bitcast(FP8X4), scales=xsc[g][:], in_=gx[g][:])
+            pieces = 2 if g == NSTEP - 1 else 1
+            wid = IMG * 256 // pieces
+            for h in range(pieces):
+                nc.vector.quantize_mx(
+                    out=xc[g][:, h * wid : (h + 1) * wid].bitcast(FP8X4),
+                    scales=xsc[g][:, h * wid : (h + 1) * wid],
+                    in_=gx[g][:, 4 * h * wid : 4 * (h + 1) * wid],
+                )
 
         def mx(g):
             if g < 0 or g >= NSTEP:
@@ -227,21 +241,26 @@ def tile_proto_t_kernel(tc, feature_map, weight2, scale, out):
 
         for g in range(LOOKAHEAD):
             load(g)
-        for k in range(NSTEP + 3):
+        for k in range(NSTEP + 6):
             load(k + LOOKAHEAD)
+            copies_w(k - 1)
+            sub(k - 3)
             quant_x(k - 1)
-            if k >= HALF and (k - HALF) % 4 == 3 and k < HALF + 12:
-                quant_wb((k - HALF) // 4 + 1)
-            sub(k - 2)
-            ccopy(k - 2)
-            dtr(k - 3)
-            sq(k - 3)
-            transp(k)
-            copies(k)
-            quant_wa(k)
-            if k == HALF - 1:
+            quant_wa(k - 1)
+            if k == HALF + 1:
                 quant_wb(0)
-            mx(k - 1)
+            if k in (HALF + 4, HALF + 8, HALF + 12):
+                quant_wb((k - HALF) // 4)
+            sq(k - 5)
+            ccopy(k - 3)
+            dtr(k - 4)
+            if k == 0:
+                transp_x(0, 0)
+            transp_w(k)
+            for i in range(1 if k == 0 else 0, IMG):
+                transp_x(k, i)
+            mx(k - 2)
+            copies_x(k)
 
         l2t = psum.tile([P, P], F32, name="l2t", tag="aux", bufs=2)
         nc.tensor.transpose(l2t[:], l2col[:], ident[:])

@@ -7,7 +7,6 @@ F32 = mybir.dt.float32
 BF16 = mybir.dt.bfloat16
 U32 = mybir.dt.uint32
 U8 = mybir.dt.uint8
-I32 = mybir.dt.int32
 FP8X4 = mybir.dt.float8_e4m3fn_x4
 ACT = mybir.ActivationFunctionType
 ALU = mybir.AluOpType
@@ -21,267 +20,261 @@ M = 512
 FLOPS = 2 * 2 * NS * NQ * D * M
 
 IMG = 4
-NSTEP = (NS + NQ) // IMG
-HALF = NS // IMG
+STEPS = (NS + NQ) // IMG
+SUPPORT_STEPS = NS // IMG
+WORDS = M // 2
+COLS = IMG * D
 LOOKAHEAD = 4
-PIN = True
-WIDTHS = (128, 128, 128, 128, 128, 128, 128, 64)
+LOGIT_DIVISOR = 800.0
 
 
 def tile_proto_t_kernel(tc, feature_map, weight2, scale, out):
     nc = tc.nc
     with ExitStack() as ctx:
-        const = ctx.enter_context(tc.tile_pool(name="const", bufs=1))
-        xpool = ctx.enter_context(tc.tile_pool(name="xpool", bufs=LOOKAHEAD + 1))
-        wpool = ctx.enter_context(tc.tile_pool(name="wpool", bufs=LOOKAHEAD + 1))
+        keep = ctx.enter_context(tc.tile_pool(name="keep", bufs=1))
+        loads = ctx.enter_context(tc.tile_pool(name="loads", bufs=LOOKAHEAD + 1))
         work = ctx.enter_context(tc.tile_pool(name="work", bufs=3))
         psum = ctx.enter_context(tc.psum_pool(name="psum", bufs=2))
 
-        ident = const.tile([P, P], F32)
+        ident = keep.tile([P, P], F32)
         make_identity(nc, ident[:])
-        sc_bf = const.tile([P, 1], BF16)
-        nc.scalar.dma_start(out=sc_bf[:], in_=scale.partition_broadcast(P))
-        a_sb = const.tile([P, 1], F32)
-        nc.vector.tensor_scalar_mul(a_sb[:], sc_bf[:], -1.0 / (800.0 * M * M))
-        l2col = const.tile([P, P], F32)
-        nc.vector.memset(l2col[:], 0.0)
-        warm = const.tile([P, 1], F32)
-        nc.scalar.activation(out=warm[:], in_=l2col[:, 0:1], func=ACT.Exp)
+        scale_bf = keep.tile([P, 1], BF16)
+        nc.scalar.dma_start(out=scale_bf[:], in_=scale.partition_broadcast(P))
+        factor = keep.tile([P, 1], F32)
+        nc.vector.tensor_scalar_mul(factor[:], scale_bf[:], -1.0 / (LOGIT_DIVISOR * M * M))
+        l2_cols = keep.tile([P, P], F32)
+        nc.vector.memset(l2_cols[:], 0.0)
+        warm = keep.tile([P, 1], F32)
+        nc.scalar.activation(out=warm[:], in_=l2_cols[:, 0:1], func=ACT.Exp)
 
-        csb = const.tile([P, 2 * NQ * NS], F32)
-        csb4 = csb[:].rearrange("p (j q s) -> p j q s", j=2, q=NQ, s=NS)
-        gb = const.tile([P, NQ * NS * 4], BF16, align_bytes=64)
-        gb4 = gb[:].bitcast(F32).rearrange("p (q s u) -> p q s u", q=NQ, s=NS, u=2)
-        wbc = const.tile([P, NQ * NS + 64], U32, align_bytes=64)
-        wbs = const.tile([P, NQ * NS + 64], U8, align_bytes=64)
-        wac = const.tile([P, NQ * NS + 64], U32, align_bytes=64)
-        was = const.tile([P, NQ * NS + 64], U8, align_bytes=64)
-        for pad in (wbc, wbs, wac, was):
-            nc.vector.memset(pad[:, NQ * NS : NQ * NS + 64].bitcast(I32), 0)
+        centroid = keep.tile([P, 2 * NQ * NS], F32)
+        centroid_jqs = centroid[:].rearrange("p (j q s) -> p j q s", j=2, q=NQ, s=NS)
+        wqs_grouped = keep.tile([P, NQ * NS * 4], BF16, align_bytes=64)
+        wqs_words = wqs_grouped[:].bitcast(F32).rearrange("p (q s u) -> p q s u", q=NQ, s=NS, u=2)
+        wqs_codes = keep.tile([P, NQ * NS], U32, align_bytes=64)
+        wqs_scales = keep.tile([P, NQ * NS], U8, align_bytes=64)
 
-        wrows = weight2.rearrange("s q m -> (s q) m").rearrange("(t p) m -> p t m", p=P)
+        weight_rows = weight2.rearrange("s q m -> (s q) m").rearrange("(t p) m -> p t m", p=P)
 
-        xs = {}
-        ws = {}
-        xt = {}
-        wt = {}
-        gx = {}
-        ga = {}
-        xc = {}
-        xsc = {}
-        mm = {}
+        feat_raw = {}
+        wgt_raw = {}
+        feat_t = {}
+        wgt_t = {}
+        feat_grouped = {}
+        wsq_grouped = {}
+        feat_codes = {}
+        feat_scales = {}
+        wsq_codes = {}
+        wsq_scales = {}
+        prod = {}
         diff = {}
-        dt = {}
+        diff_t = {}
 
         def load(g):
-            if g >= NSTEP:
+            if g >= STEPS:
                 return
-            xs[g] = xpool.tile([P, IMG * 1024], BF16, name="xs", tag="xs")
-            dst = xs[g][:].rearrange("p (i f) -> p i f", i=IMG)
+            feat_raw[g] = loads.tile([P, IMG * 2 * M], BF16, name="feat_raw", tag="feat_raw")
+            dst = feat_raw[g][:].rearrange("p (i f) -> p i f", i=IMG)
             src = feature_map[IMG * g : IMG * (g + 1)].rearrange("i (p j) m -> p i (j m)", j=2)
-            if g == 0 or g == NSTEP - 1:
+            if g == 0:
                 nc.sync.dma_start(out=dst[:, 0, :], in_=src[:, 0, :])
-            if g < HALF:
-                ws[g] = wpool.tile([P, 2 * M], BF16, name="ws", tag="ws")
+            if g < SUPPORT_STEPS:
+                wgt_raw[g] = loads.tile([P, 2 * M], BF16, name="wgt_raw", tag="wgt_raw")
                 nc.sync.dma_start(
-                    out=ws[g][:].rearrange("p (t m) -> p t m", t=2), in_=wrows[:, 2 * g : 2 * g + 2, :]
+                    out=wgt_raw[g][:].rearrange("p (t m) -> p t m", t=2), in_=weight_rows[:, 2 * g : 2 * g + 2, :]
                 )
-            if g == 0 or g == NSTEP - 1:
-                for i in range(1, IMG):
-                    nc.sync.dma_start(out=dst[:, i, :], in_=src[:, i, :])
+            if g == 0:
+                nc.sync.dma_start(out=dst[:, 1:IMG, :], in_=src[:, 1:IMG, :])
             else:
                 nc.sync.dma_start(out=dst, in_=src)
 
-        def transp_w(g):
-            if g >= HALF:
+        def transpose_weights(g):
+            if g >= SUPPORT_STEPS:
                 return
-            wt[g] = psum.tile([P, 2, 256], F32, name="wt", tag="aux", bufs=2)
-            ww = ws[g][:].bitcast(F32)
+            wgt_t[g] = psum.tile([P, 2, 2 * P], F32, name="wgt_t", tag="small", bufs=2)
+            words = wgt_raw[g][:].bitcast(F32)
             for t in range(2):
                 for u in range(2):
-                    nc.tensor.transpose(
-                        wt[g][:, u, t * P : (t + 1) * P], ww[:, t * 256 + u * P : t * 256 + (u + 1) * P], ident[:]
-                    )
+                    w0 = t * WORDS + u * P
+                    nc.tensor.transpose(wgt_t[g][:, u, t * P : (t + 1) * P], words[:, w0 : w0 + P], ident[:])
 
-        def transp_x(g, i):
-            if g >= NSTEP:
+        def transpose_image(g, i):
+            if g >= STEPS:
                 return
-            xw = xs[g][:].bitcast(F32)
-            xt[g, i] = psum.tile([P, 2, 256], F32, name="xt", tag="xt", bufs=4)
+            feat_t[g, i] = psum.tile([P, 2, D], F32, name="feat_t", tag="feat_t", bufs=IMG)
+            words = feat_raw[g][:].bitcast(F32)
             for j in range(2):
                 for u in range(2):
-                    c0 = i * 512 + j * 256 + u * P
-                    nc.tensor.transpose(xt[g, i][:, u, j * P : (j + 1) * P], xw[:, c0 : c0 + P], ident[:])
+                    w0 = (i * 2 + j) * WORDS + u * P
+                    nc.tensor.transpose(feat_t[g, i][:, u, j * P : (j + 1) * P], words[:, w0 : w0 + P], ident[:])
 
-        def copy_x(g, i, on_vector):
-            dst = gx[g][:].bitcast(F32)[:, i * 512 : (i + 1) * 512].rearrange("p (c u) -> p c u", u=2)
-            src = xt[g, i][:].rearrange("p u c -> p c u")
-            if on_vector:
-                nc.vector.tensor_copy(out=dst, in_=src)
-            else:
-                nc.scalar.copy(out=dst, in_=src)
-
-        def copies_w(g):
-            if g < 0 or g >= HALF:
+        def group_weights(g):
+            if g < 0 or g >= SUPPORT_STEPS:
                 return
-            ga[g] = work.tile([P, 1024], BF16, name="ga", tag="ga", align_bytes=64)
+            wsq_grouped[g] = work.tile([P, IMG * NQ * 4], BF16, name="wsq_grouped", tag="wsq_grouped", align_bytes=64)
             nc.vector.tensor_copy(
-                out=ga[g][:].bitcast(F32).rearrange("p (c u) -> p c u", u=2),
-                in_=wt[g][:].rearrange("p u c -> p c u"),
+                out=wsq_grouped[g][:].bitcast(F32).rearrange("p (c u) -> p c u", u=2),
+                in_=wgt_t[g][:].rearrange("p u c -> p c u"),
             )
             nc.vector.tensor_copy(
-                out=gb4[:, :, IMG * g : IMG * (g + 1), :],
-                in_=wt[g][:].rearrange("p u (s q) -> p q s u", s=IMG, q=NQ),
+                out=wqs_words[:, :, IMG * g : IMG * (g + 1), :],
+                in_=wgt_t[g][:].rearrange("p u (s q) -> p q s u", s=IMG, q=NQ),
             )
 
-        def copies_x(g):
-            if g >= NSTEP:
+        def group_images(g):
+            if g >= STEPS:
                 return
-            gx[g] = work.tile([P, IMG * 1024], BF16, name="gx", tag="gx", align_bytes=64)
+            feat_grouped[g] = work.tile([P, COLS * 4], BF16, name="feat_grouped", tag="feat_grouped", align_bytes=64)
+            words = feat_grouped[g][:].bitcast(F32)
             for i in range(IMG):
-                if g == NSTEP - 1:
-                    copy_x(g, i, i % 2 == 1)
+                dst = words[:, i * 2 * D : (i + 1) * 2 * D].rearrange("p (c u) -> p c u", u=2)
+                src = feat_t[g, i][:].rearrange("p u c -> p c u")
+                if g == STEPS - 1:
+                    on_vector = i % 2 == 1
                 else:
-                    copy_x(g, i, g >= HALF and i == IMG - 1)
+                    on_vector = g >= SUPPORT_STEPS and i == IMG - 1
+                if on_vector:
+                    nc.vector.tensor_copy(out=dst, in_=src)
+                else:
+                    nc.scalar.copy(out=dst, in_=src)
 
-        def quant_wa(g):
-            if g < 0 or g >= HALF:
+        def quantise_images(g):
+            if g < 0 or g >= STEPS:
                 return
-            nc.vector.quantize_mx(
-                out=wac[:, 256 * g : 256 * (g + 1)].bitcast(FP8X4), scales=was[:, 256 * g : 256 * (g + 1)], in_=ga[g][:]
-            )
-
-        def quant_wb(k):
-            nc.vector.quantize_mx(
-                out=wbc[:, k * 1024 : (k + 1) * 1024].bitcast(FP8X4),
-                scales=wbs[:, k * 1024 : (k + 1) * 1024],
-                in_=gb[:, k * 4096 : (k + 1) * 4096],
-            )
-
-        def quant_x(g):
-            if g < 0 or g >= NSTEP:
-                return
-            xc[g] = work.tile([P, IMG * 256], U32, name="xc", tag="xc", align_bytes=64)
-            xsc[g] = work.tile([P, IMG * 256], U8, name="xsc", tag="xsc", align_bytes=64)
-            pieces = 2 if g == NSTEP - 1 else 1
-            wid = IMG * 256 // pieces
+            feat_codes[g] = work.tile([P, COLS], U32, name="feat_codes", tag="feat_codes", align_bytes=64)
+            feat_scales[g] = work.tile([P, COLS], U8, name="feat_scales", tag="feat_scales", align_bytes=64)
+            pieces = 2 if g == STEPS - 1 else 1
+            width = COLS // pieces
             for h in range(pieces):
                 nc.vector.quantize_mx(
-                    out=xc[g][:, h * wid : (h + 1) * wid].bitcast(FP8X4),
-                    scales=xsc[g][:, h * wid : (h + 1) * wid],
-                    in_=gx[g][:, 4 * h * wid : 4 * (h + 1) * wid],
+                    out=feat_codes[g][:, h * width : (h + 1) * width].bitcast(FP8X4),
+                    scales=feat_scales[g][:, h * width : (h + 1) * width],
+                    in_=feat_grouped[g][:, 4 * h * width : 4 * (h + 1) * width],
                 )
 
-        def mx(g):
-            if g < 0 or g >= NSTEP:
+        def quantise_weights_sq(g):
+            if g < 0 or g >= SUPPORT_STEPS:
                 return
-            mm[g] = psum.tile([P, 512], F32, name="mm", tag="mm", bufs=2)
-            for slot in range(8):
-                if g < HALF:
-                    j, i = slot // IMG, slot % IMG
-                    codes, planes = wac, was
-                else:
-                    i, j = (slot // 4) * 2 + slot % 2, (slot // 2) % 2
-                    codes, planes = wbc, wbs
-                c0 = i * 256 + j * P
-                w0 = (IMG * (g % HALF) + i) * 64
-                n = WIDTHS[slot]
-                nc.tensor.matmul_mx(
-                    out=mm[g][:, slot * 64 : slot * 64 + n],
-                    lhsT=xc[g][:, c0 : c0 + P].bitcast(FP8X4),
-                    lhsT_scale=xsc[g][:, c0 : c0 + P],
-                    rhs=codes[:, w0 : w0 + n].bitcast(FP8X4),
-                    rhs_scale=planes[:, w0 : w0 + n],
-                    start=True,
-                    stop=True,
-                )
+            wsq_codes[g] = work.tile([P, IMG * NQ], U32, name="wsq_codes", tag="wsq_codes", align_bytes=64)
+            wsq_scales[g] = work.tile([P, IMG * NQ], U8, name="wsq_scales", tag="wsq_scales", align_bytes=64)
+            nc.vector.quantize_mx(out=wsq_codes[g][:].bitcast(FP8X4), scales=wsq_scales[g][:], in_=wsq_grouped[g][:])
 
-        def ccopy(g):
-            if g < 0 or g >= HALF:
-                return
-            nc.scalar.copy(
-                out=csb4[:, :, :, IMG * g : IMG * (g + 1)],
-                in_=mm[g][:].rearrange("p (j i q) -> p j q i", j=2, i=IMG, q=NQ),
+        def quantise_weights_qs(quarter):
+            c0, c1 = quarter * 1024, (quarter + 1) * 1024
+            nc.vector.quantize_mx(
+                out=wqs_codes[:, c0:c1].bitcast(FP8X4), scales=wqs_scales[:, c0:c1], in_=wqs_grouped[:, 4 * c0 : 4 * c1]
             )
 
-        def sub(g):
-            if g < HALF or g >= NSTEP:
+        def multiply(g):
+            if g < 0 or g >= STEPS:
                 return
-            h = g - HALF
-            diff[g] = work.tile([P, 512], F32, name="diff", tag="diff")
+            prod[g] = psum.tile([P, 8 * 64], F32, name="prod", tag="prod", bufs=2)
+            for i in range(IMG):
+                for j in range(2):
+                    c0 = i * D + j * P
+                    if g < SUPPORT_STEPS:
+                        slot = j * IMG + i
+                        rhs = wsq_codes[g][:, i * NQ : (i + 1) * NQ]
+                        rhs_scale = wsq_scales[g][:, i * NQ : (i + 1) * NQ]
+                    else:
+                        slot = (i // 2) * 4 + j * 2 + i % 2
+                        q = IMG * (g - SUPPORT_STEPS) + i
+                        rhs = wqs_codes[:, q * NS : (q + 1) * NS]
+                        rhs_scale = wqs_scales[:, q * NS : (q + 1) * NS]
+                    nc.tensor.matmul_mx(
+                        out=prod[g][:, slot * 64 : (slot + 1) * 64],
+                        lhsT=feat_codes[g][:, c0 : c0 + P].bitcast(FP8X4),
+                        lhsT_scale=feat_scales[g][:, c0 : c0 + P],
+                        rhs=rhs.bitcast(FP8X4),
+                        rhs_scale=rhs_scale,
+                        start=True,
+                        stop=True,
+                    )
+
+        def park_centroid(g):
+            if g < 0 or g >= SUPPORT_STEPS:
+                return
+            nc.scalar.copy(
+                out=centroid_jqs[:, :, :, IMG * g : IMG * (g + 1)],
+                in_=prod[g][:].rearrange("p (j i q) -> p j q i", j=2, i=IMG, q=NQ),
+            )
+
+        def subtract(g):
+            if g < SUPPORT_STEPS or g >= STEPS:
+                return
+            q0 = IMG * (g - SUPPORT_STEPS)
+            diff[g] = work.tile([P, 8 * 64], F32, name="diff", tag="diff")
             nc.vector.tensor_tensor(
                 out=diff[g][:].rearrange("p (a j f) -> p a j f", a=2, j=2),
-                in0=mm[g][:].rearrange("p (a j f) -> p a j f", a=2, j=2),
-                in1=csb4[:, :, IMG * h : IMG * (h + 1), :].rearrange("p j (a b) s -> p a j (b s)", a=2, b=2),
+                in0=prod[g][:].rearrange("p (a j f) -> p a j f", a=2, j=2),
+                in1=centroid_jqs[:, :, q0 : q0 + IMG, :].rearrange("p j (a b) s -> p a j (b s)", a=2, b=2),
                 op=ALU.subtract,
             )
 
-        def dtr(g):
-            if g < HALF or g >= NSTEP:
+        def transpose_diff(g):
+            if g < SUPPORT_STEPS or g >= STEPS:
                 return
-            dt[g] = psum.tile([P, 512], F32, name="dt", tag="aux", bufs=2)
+            diff_t[g] = psum.tile([P, 4 * P], F32, name="diff_t", tag="small", bufs=2)
             for b in range(4):
-                nc.tensor.transpose(dt[g][:, b * P : (b + 1) * P], diff[g][:, b * P : (b + 1) * P], ident[:])
+                nc.tensor.transpose(diff_t[g][:, b * P : (b + 1) * P], diff[g][:, b * P : (b + 1) * P], ident[:])
 
-        def sq(g):
-            if g < HALF or g >= NSTEP:
+        def square_and_sum(g):
+            if g < SUPPORT_STEPS or g >= STEPS:
                 return
-            h = g - HALF
             for a in range(2):
-                junk = work.tile([P, 256], F32, name="junk", tag="junk")
+                pair = 2 * (g - SUPPORT_STEPS) + a
+                squares = work.tile([P, D], F32, name="squares", tag="squares")
                 nc.scalar.activation(
-                    out=junk[:],
-                    in_=dt[g][:, a * 256 : (a + 1) * 256],
+                    out=squares[:],
+                    in_=diff_t[g][:, a * D : (a + 1) * D],
                     func=ACT.Square,
-                    accum_out=l2col[:, 2 * h + a : 2 * h + a + 1],
+                    accum_out=l2_cols[:, pair : pair + 1],
                 )
 
-        if PIN:
-            ctx.enter_context(tc.manual_schedule())
-
+        ctx.enter_context(tc.manual_schedule())
         for g in range(LOOKAHEAD):
             load(g)
-        for k in range(NSTEP + 6):
+        for k in range(STEPS + 6):
             load(k + LOOKAHEAD)
-            copies_w(k - 1)
-            sub(k - 3)
-            quant_x(k - 1)
-            quant_wa(k - 1)
-            if k == HALF + 1:
-                quant_wb(0)
-            if k in (HALF + 4, HALF + 8, HALF + 12):
-                quant_wb((k - HALF) // 4)
-            sq(k - 5)
-            ccopy(k - 3)
-            dtr(k - 4)
+            group_weights(k - 1)
+            subtract(k - 3)
+            quantise_images(k - 1)
+            quantise_weights_sq(k - 1)
+            if k == SUPPORT_STEPS + 1:
+                quantise_weights_qs(0)
+            if k in (SUPPORT_STEPS + 4, SUPPORT_STEPS + 8, SUPPORT_STEPS + 12):
+                quantise_weights_qs((k - SUPPORT_STEPS) // 4)
+            square_and_sum(k - 5)
+            park_centroid(k - 3)
+            transpose_diff(k - 4)
             if k == 0:
-                transp_x(0, 0)
-            transp_w(k)
+                transpose_image(0, 0)
+            transpose_weights(k)
             for i in range(1 if k == 0 else 0, IMG):
-                transp_x(k, i)
-            mx(k - 2)
-            copies_x(k)
+                transpose_image(k, i)
+            multiply(k - 2)
+            group_images(k)
 
-        l2t = psum.tile([P, P], F32, name="l2t", tag="aux", bufs=2)
-        nc.tensor.transpose(l2t[:], l2col[:], ident[:])
-        lg = const.tile([P, 2, NS], F32)
-        nc.vector.tensor_scalar_mul(lg[:].rearrange("p a s -> p (a s)"), l2t[:], a_sb[:, 0:1])
-        top = const.tile([P, 2], F32)
-        nc.vector.tensor_reduce(out=top[:], in_=lg[:], axis=AX.X, op=ALU.max)
-        z = const.tile([P, 2, NS], F32)
+        l2_rows = psum.tile([P, P], F32, name="l2_rows", tag="small", bufs=2)
+        nc.tensor.transpose(l2_rows[:], l2_cols[:], ident[:])
+        logits = keep.tile([P, 2, NS], F32)
+        nc.vector.tensor_scalar_mul(logits[:].rearrange("p a s -> p (a s)"), l2_rows[:], factor[:, 0:1])
+        top = keep.tile([P, 2], F32)
+        nc.vector.tensor_reduce(out=top[:], in_=logits[:], axis=AX.X, op=ALU.max)
+        shifted = keep.tile([P, 2, NS], F32)
         nc.vector.tensor_tensor(
-            out=z[:], in0=lg[:], in1=top[:].unsqueeze(2).to_broadcast([P, 2, NS]), op=ALU.subtract
+            out=shifted[:], in0=logits[:], in1=top[:].unsqueeze(2).to_broadcast([P, 2, NS]), op=ALU.subtract
         )
-        ez = const.tile([P, 2, NS], F32)
-        tot = const.tile([P, 2], F32)
+        exps = keep.tile([P, 2, NS], F32)
+        total = keep.tile([P, 2], F32)
         for a in range(2):
-            nc.scalar.activation(out=ez[:, a, :], in_=z[:, a, :], func=ACT.Exp, accum_out=tot[:, a : a + 1])
-        ltot = const.tile([P, 2], F32)
-        nc.scalar.activation(out=ltot[:], in_=tot[:], func=ACT.Ln)
-        res = const.tile([P, 2, NS], F32)
+            nc.scalar.activation(out=exps[:, a, :], in_=shifted[:, a, :], func=ACT.Exp, accum_out=total[:, a : a + 1])
+        log_total = keep.tile([P, 2], F32)
+        nc.scalar.activation(out=log_total[:], in_=total[:], func=ACT.Ln)
+        result = keep.tile([P, 2, NS], F32)
         nc.vector.tensor_tensor(
-            out=res[:], in0=z[:], in1=ltot[:].unsqueeze(2).to_broadcast([P, 2, NS]), op=ALU.subtract
+            out=result[:], in0=shifted[:], in1=log_total[:].unsqueeze(2).to_broadcast([P, 2, NS]), op=ALU.subtract
         )
         nc.sync.dma_start(
-            out=out.rearrange("(u a) s -> u (a s)", a=2), in_=res[0:32].rearrange("p a s -> p (a s)")
+            out=out.rearrange("(u a) s -> u (a s)", a=2), in_=result[0 : NQ // 2].rearrange("p a s -> p (a s)")
         )

@@ -7,6 +7,7 @@ F32 = mybir.dt.float32
 BF16 = mybir.dt.bfloat16
 U32 = mybir.dt.uint32
 U8 = mybir.dt.uint8
+I32 = mybir.dt.int32
 FP8X4 = mybir.dt.float8_e4m3fn_x4
 ACT = mybir.ActivationFunctionType
 ALU = mybir.AluOpType
@@ -20,261 +21,278 @@ M = 512
 FLOPS = 2 * 2 * NS * NQ * D * M
 
 IMG = 4
-STEPS = (NS + NQ) // IMG
-SUPPORT_STEPS = NS // IMG
-WORDS = M // 2
-COLS = IMG * D
+NSTEP = (NS + NQ) // IMG
+HALF = NS // IMG
 LOOKAHEAD = 4
-LOGIT_DIVISOR = 800.0
+PIN = True
+WIDTHS = (128, 128, 128, 128, 128, 128, 128, 64)
 
 
 def tile_proto_t_kernel(tc, feature_map, weight2, scale, out):
     nc = tc.nc
     with ExitStack() as ctx:
-        keep = ctx.enter_context(tc.tile_pool(name="keep", bufs=1))
-        loads = ctx.enter_context(tc.tile_pool(name="loads", bufs=LOOKAHEAD + 1))
+        const = ctx.enter_context(tc.tile_pool(name="const", bufs=1))
+        xpool = ctx.enter_context(tc.tile_pool(name="xpool", bufs=LOOKAHEAD + 1))
+        wpool = ctx.enter_context(tc.tile_pool(name="wpool", bufs=LOOKAHEAD + 1))
         work = ctx.enter_context(tc.tile_pool(name="work", bufs=3))
         psum = ctx.enter_context(tc.psum_pool(name="psum", bufs=2))
 
-        ident = keep.tile([P, P], F32)
+        ident = const.tile([P, P], F32)
         make_identity(nc, ident[:])
-        scale_bf = keep.tile([P, 1], BF16)
-        nc.scalar.dma_start(out=scale_bf[:], in_=scale.partition_broadcast(P))
-        factor = keep.tile([P, 1], F32)
-        nc.vector.tensor_scalar_mul(factor[:], scale_bf[:], -1.0 / (LOGIT_DIVISOR * M * M))
-        l2_cols = keep.tile([P, P], F32)
-        nc.vector.memset(l2_cols[:], 0.0)
-        warm = keep.tile([P, 1], F32)
-        nc.scalar.activation(out=warm[:], in_=l2_cols[:, 0:1], func=ACT.Exp)
+        sc_bf = const.tile([P, 1], BF16)
+        nc.scalar.dma_start(out=sc_bf[:], in_=scale.partition_broadcast(P))
+        a_sb = const.tile([P, 1], F32)
+        nc.vector.tensor_scalar_mul(a_sb[:], sc_bf[:], -1.0 / (800.0 * M * M))
+        l2col = const.tile([P, P], F32)
+        nc.vector.memset(l2col[:], 0.0)
+        warm = const.tile([P, 1], F32)
+        nc.scalar.activation(out=warm[:], in_=l2col[:, 0:1], func=ACT.Exp)
 
-        centroid = keep.tile([P, 2 * NQ * NS], F32)
-        centroid_jqs = centroid[:].rearrange("p (j q s) -> p j q s", j=2, q=NQ, s=NS)
-        wqs_grouped = keep.tile([P, NQ * NS * 4], BF16, align_bytes=64)
-        wqs_words = wqs_grouped[:].bitcast(F32).rearrange("p (q s u) -> p q s u", q=NQ, s=NS, u=2)
-        wqs_codes = keep.tile([P, NQ * NS], U32, align_bytes=64)
-        wqs_scales = keep.tile([P, NQ * NS], U8, align_bytes=64)
+        csb = const.tile([P, 2 * NQ * NS], F32)
+        csb4 = csb[:].rearrange("p (j q s) -> p j q s", j=2, q=NQ, s=NS)
+        gb = const.tile([P, NQ * NS * 4], BF16, align_bytes=64)
+        gb4 = gb[:].bitcast(F32).rearrange("p (q s u) -> p q s u", q=NQ, s=NS, u=2)
+        wbc = const.tile([P, NQ * NS + 64], U32, align_bytes=64)
+        wbs = const.tile([P, NQ * NS + 64], U8, align_bytes=64)
+        wac = const.tile([P, NQ * NS + 64], U32, align_bytes=64)
+        was = const.tile([P, NQ * NS + 64], U8, align_bytes=64)
+        for pad in (wbc, wbs, wac, was):
+            nc.vector.memset(pad[:, NQ * NS : NQ * NS + 64].bitcast(I32), 0)
 
-        weight_rows = weight2.rearrange("s q m -> (s q) m").rearrange("(t p) m -> p t m", p=P)
+        wrows = weight2.rearrange("s q m -> (s q) m").rearrange("(t p) m -> p t m", p=P)
 
-        feat_raw = {}
-        wgt_raw = {}
-        feat_t = {}
-        wgt_t = {}
-        feat_grouped = {}
-        wsq_grouped = {}
-        feat_codes = {}
-        feat_scales = {}
-        wsq_codes = {}
-        wsq_scales = {}
-        prod = {}
+        xs = {}
+        ws = {}
+        xt = {}
+        wt = {}
+        gx = {}
+        ga = {}
+        xc = {}
+        xsc = {}
+        mm = {}
         diff = {}
-        diff_t = {}
+        dt = {}
 
         def load(g):
-            if g >= STEPS:
+            if g >= NSTEP:
                 return
-            feat_raw[g] = loads.tile([P, IMG * 2 * M], BF16, name="feat_raw", tag="feat_raw")
-            dst = feat_raw[g][:].rearrange("p (i f) -> p i f", i=IMG)
-            src = feature_map[IMG * g : IMG * (g + 1)].rearrange("i (p j) m -> p i (j m)", j=2)
+            xs[g] = xpool.tile([P, IMG * 1024], BF16, name="xs", tag="xs")
+            dst = xs[g][:].rearrange("p (b f) -> p b f", b=IMG)
+            src = (
+                feature_map[IMG * g : IMG * (g + 1)]
+                .rearrange("i d m -> (i d) m")
+                .rearrange("(p b r) m -> p b (r m)", b=IMG, r=2)
+            )
             if g == 0:
                 nc.sync.dma_start(out=dst[:, 0, :], in_=src[:, 0, :])
-            if g < SUPPORT_STEPS:
-                wgt_raw[g] = loads.tile([P, 2 * M], BF16, name="wgt_raw", tag="wgt_raw")
+            if g < HALF:
+                ws[g] = wpool.tile([P, 2 * M], BF16, name="ws", tag="ws")
                 nc.sync.dma_start(
-                    out=wgt_raw[g][:].rearrange("p (t m) -> p t m", t=2), in_=weight_rows[:, 2 * g : 2 * g + 2, :]
+                    out=ws[g][:].rearrange("p (t m) -> p t m", t=2), in_=wrows[:, 2 * g : 2 * g + 2, :]
                 )
             if g == 0:
-                nc.sync.dma_start(out=dst[:, 1:IMG, :], in_=src[:, 1:IMG, :])
+                for i in range(1, IMG):
+                    nc.sync.dma_start(out=dst[:, i, :], in_=src[:, i, :])
             else:
-                nc.sync.dma_start(out=dst, in_=src)
-
-        def transpose_weights(g):
-            if g >= SUPPORT_STEPS:
-                return
-            wgt_t[g] = psum.tile([P, 2, 2 * P], F32, name="wgt_t", tag="small", bufs=2)
-            words = wgt_raw[g][:].bitcast(F32)
-            for t in range(2):
-                for u in range(2):
-                    w0 = t * WORDS + u * P
-                    nc.tensor.transpose(wgt_t[g][:, u, t * P : (t + 1) * P], words[:, w0 : w0 + P], ident[:])
-
-        def transpose_image(g, i):
-            if g >= STEPS:
-                return
-            feat_t[g, i] = psum.tile([P, 2, D], F32, name="feat_t", tag="feat_t", bufs=IMG)
-            words = feat_raw[g][:].bitcast(F32)
-            for j in range(2):
-                for u in range(2):
-                    w0 = (i * 2 + j) * WORDS + u * P
-                    nc.tensor.transpose(feat_t[g, i][:, u, j * P : (j + 1) * P], words[:, w0 : w0 + P], ident[:])
-
-        def group_weights(g):
-            if g < 0 or g >= SUPPORT_STEPS:
-                return
-            wsq_grouped[g] = work.tile([P, IMG * NQ * 4], BF16, name="wsq_grouped", tag="wsq_grouped", align_bytes=64)
-            nc.vector.tensor_copy(
-                out=wsq_grouped[g][:].bitcast(F32).rearrange("p (c u) -> p c u", u=2),
-                in_=wgt_t[g][:].rearrange("p u c -> p c u"),
-            )
-            nc.vector.tensor_copy(
-                out=wqs_words[:, :, IMG * g : IMG * (g + 1), :],
-                in_=wgt_t[g][:].rearrange("p u (s q) -> p q s u", s=IMG, q=NQ),
-            )
-
-        def group_images(g):
-            if g >= STEPS:
-                return
-            feat_grouped[g] = work.tile([P, COLS * 4], BF16, name="feat_grouped", tag="feat_grouped", align_bytes=64)
-            words = feat_grouped[g][:].bitcast(F32)
-            for i in range(IMG):
-                dst = words[:, i * 2 * D : (i + 1) * 2 * D].rearrange("p (c u) -> p c u", u=2)
-                src = feat_t[g, i][:].rearrange("p u c -> p c u")
-                if g == STEPS - 1:
-                    on_vector = i % 2 == 1
-                else:
-                    on_vector = g >= SUPPORT_STEPS and i == IMG - 1
-                if on_vector:
-                    nc.vector.tensor_copy(out=dst, in_=src)
-                else:
-                    nc.scalar.copy(out=dst, in_=src)
-
-        def quantise_images(g):
-            if g < 0 or g >= STEPS:
-                return
-            feat_codes[g] = work.tile([P, COLS], U32, name="feat_codes", tag="feat_codes", align_bytes=64)
-            feat_scales[g] = work.tile([P, COLS], U8, name="feat_scales", tag="feat_scales", align_bytes=64)
-            pieces = 2 if g == STEPS - 1 else 1
-            width = COLS // pieces
-            for h in range(pieces):
-                nc.vector.quantize_mx(
-                    out=feat_codes[g][:, h * width : (h + 1) * width].bitcast(FP8X4),
-                    scales=feat_scales[g][:, h * width : (h + 1) * width],
-                    in_=feat_grouped[g][:, 4 * h * width : 4 * (h + 1) * width],
+                nc.sync.dma_start(
+                    out=xs[g][:],
+                    in_=feature_map[IMG * g : IMG * (g + 1)]
+                    .rearrange("i d m -> (i d) m")
+                    .rearrange("(p r) m -> p (r m)", r=2 * IMG),
                 )
 
-        def quantise_weights_sq(g):
-            if g < 0 or g >= SUPPORT_STEPS:
+        def transp_w(g):
+            if g >= HALF:
                 return
-            wsq_codes[g] = work.tile([P, IMG * NQ], U32, name="wsq_codes", tag="wsq_codes", align_bytes=64)
-            wsq_scales[g] = work.tile([P, IMG * NQ], U8, name="wsq_scales", tag="wsq_scales", align_bytes=64)
-            nc.vector.quantize_mx(out=wsq_codes[g][:].bitcast(FP8X4), scales=wsq_scales[g][:], in_=wsq_grouped[g][:])
-
-        def quantise_weights_qs(quarter):
-            c0, c1 = quarter * 1024, (quarter + 1) * 1024
-            nc.vector.quantize_mx(
-                out=wqs_codes[:, c0:c1].bitcast(FP8X4), scales=wqs_scales[:, c0:c1], in_=wqs_grouped[:, 4 * c0 : 4 * c1]
-            )
-
-        def multiply(g):
-            if g < 0 or g >= STEPS:
-                return
-            prod[g] = psum.tile([P, 8 * 64], F32, name="prod", tag="prod", bufs=2)
-            for i in range(IMG):
-                for j in range(2):
-                    c0 = i * D + j * P
-                    if g < SUPPORT_STEPS:
-                        slot = j * IMG + i
-                        rhs = wsq_codes[g][:, i * NQ : (i + 1) * NQ]
-                        rhs_scale = wsq_scales[g][:, i * NQ : (i + 1) * NQ]
-                    else:
-                        slot = (i // 2) * 4 + j * 2 + i % 2
-                        q = IMG * (g - SUPPORT_STEPS) + i
-                        rhs = wqs_codes[:, q * NS : (q + 1) * NS]
-                        rhs_scale = wqs_scales[:, q * NS : (q + 1) * NS]
-                    nc.tensor.matmul_mx(
-                        out=prod[g][:, slot * 64 : (slot + 1) * 64],
-                        lhsT=feat_codes[g][:, c0 : c0 + P].bitcast(FP8X4),
-                        lhsT_scale=feat_scales[g][:, c0 : c0 + P],
-                        rhs=rhs.bitcast(FP8X4),
-                        rhs_scale=rhs_scale,
-                        start=True,
-                        stop=True,
+            wt[g] = psum.tile([P, 2, 256], F32, name="wt", tag="aux", bufs=2)
+            ww = ws[g][:].bitcast(F32)
+            for t in range(2):
+                for u in range(2):
+                    nc.tensor.transpose(
+                        wt[g][:, u, t * P : (t + 1) * P], ww[:, t * 256 + u * P : t * 256 + (u + 1) * P], ident[:]
                     )
 
-        def park_centroid(g):
-            if g < 0 or g >= SUPPORT_STEPS:
+        def transp_x(g, i):
+            if g >= NSTEP:
                 return
-            nc.scalar.copy(
-                out=centroid_jqs[:, :, :, IMG * g : IMG * (g + 1)],
-                in_=prod[g][:].rearrange("p (j i q) -> p j q i", j=2, i=IMG, q=NQ),
+            xw = xs[g][:].bitcast(F32)
+            xt[g, i] = psum.tile([P, 2, IMG, 2, 32], F32, name="xt", tag="xt", bufs=4)
+            for j in range(2):
+                for u in range(2):
+                    c0 = i * 512 + j * 256 + u * P
+                    nc.tensor.transpose(
+                        xt[g, i][:, u, :, j, :], xw[:, c0 : c0 + P], ident[:].rearrange("p (i c) -> p i c", i=IMG)
+                    )
+
+        def copy_x(g, i, on_vector):
+            dst = gx[g][:].bitcast(F32).rearrange("p (i b c u) -> p i b c u", i=IMG, b=IMG, c=64, u=2)[:, :, i, :, :]
+            src = xt[g, i][:].rearrange("p u i r c -> p i (r c) u")
+            if on_vector:
+                nc.vector.tensor_copy(out=dst, in_=src)
+            else:
+                nc.scalar.copy(out=dst, in_=src)
+
+        def copies_w(g):
+            if g < 0 or g >= HALF:
+                return
+            ga[g] = work.tile([P, 1024], BF16, name="ga", tag="ga", align_bytes=64)
+            nc.vector.tensor_copy(
+                out=ga[g][:].bitcast(F32).rearrange("p (c u) -> p c u", u=2),
+                in_=wt[g][:].rearrange("p u c -> p c u"),
+            )
+            nc.vector.tensor_copy(
+                out=gb4[:, :, IMG * g : IMG * (g + 1), :],
+                in_=wt[g][:].rearrange("p u (s q) -> p q s u", s=IMG, q=NQ),
             )
 
-        def subtract(g):
-            if g < SUPPORT_STEPS or g >= STEPS:
+        def copies_x(g):
+            if g >= NSTEP:
                 return
-            q0 = IMG * (g - SUPPORT_STEPS)
-            diff[g] = work.tile([P, 8 * 64], F32, name="diff", tag="diff")
+            gx[g] = work.tile([P, IMG * 1024], BF16, name="gx", tag="gx", align_bytes=64)
+            for i in range(IMG):
+                if g == NSTEP - 1:
+                    copy_x(g, i, i % 2 == 1)
+                else:
+                    copy_x(g, i, g >= HALF and i == IMG - 1)
+
+        def quant_wa(g):
+            if g < 0 or g >= HALF:
+                return
+            nc.vector.quantize_mx(
+                out=wac[:, 256 * g : 256 * (g + 1)].bitcast(FP8X4), scales=was[:, 256 * g : 256 * (g + 1)], in_=ga[g][:]
+            )
+
+        def quant_wb(k):
+            nc.vector.quantize_mx(
+                out=wbc[:, k * 1024 : (k + 1) * 1024].bitcast(FP8X4),
+                scales=wbs[:, k * 1024 : (k + 1) * 1024],
+                in_=gb[:, k * 4096 : (k + 1) * 4096],
+            )
+
+        def quant_x(g):
+            if g < 0 or g >= NSTEP:
+                return
+            xc[g] = work.tile([P, IMG * 256], U32, name="xc", tag="xc", align_bytes=64)
+            xsc[g] = work.tile([P, IMG * 256], U8, name="xsc", tag="xsc", align_bytes=64)
+            pieces = 1
+            wid = IMG * 256 // pieces
+            for h in range(pieces):
+                nc.vector.quantize_mx(
+                    out=xc[g][:, h * wid : (h + 1) * wid].bitcast(FP8X4),
+                    scales=xsc[g][:, h * wid : (h + 1) * wid],
+                    in_=gx[g][:, 4 * h * wid : 4 * (h + 1) * wid],
+                )
+
+        def mx(g):
+            if g < 0 or g >= NSTEP:
+                return
+            mm[g] = psum.tile([P, 512], F32, name="mm", tag="mm", bufs=2)
+            for slot in range(8):
+                if g < HALF:
+                    j, i = slot // IMG, slot % IMG
+                    codes, planes = wac, was
+                else:
+                    i, j = (slot // 4) * 2 + slot % 2, (slot // 2) % 2
+                    codes, planes = wbc, wbs
+                c0 = i * 256 + j * P
+                w0 = (IMG * (g % HALF) + i) * 64
+                n = WIDTHS[slot]
+                nc.tensor.matmul_mx(
+                    out=mm[g][:, slot * 64 : slot * 64 + n],
+                    lhsT=xc[g][:, c0 : c0 + P].bitcast(FP8X4),
+                    lhsT_scale=xsc[g][:, c0 : c0 + P],
+                    rhs=codes[:, w0 : w0 + n].bitcast(FP8X4),
+                    rhs_scale=planes[:, w0 : w0 + n],
+                    start=True,
+                    stop=True,
+                )
+
+        def ccopy(g):
+            if g < 0 or g >= HALF:
+                return
+            nc.scalar.copy(
+                out=csb4[:, :, :, IMG * g : IMG * (g + 1)],
+                in_=mm[g][:].rearrange("p (j i q) -> p j q i", j=2, i=IMG, q=NQ),
+            )
+
+        def sub(g):
+            if g < HALF or g >= NSTEP:
+                return
+            h = g - HALF
+            diff[g] = work.tile([P, 512], F32, name="diff", tag="diff")
             nc.vector.tensor_tensor(
                 out=diff[g][:].rearrange("p (a j f) -> p a j f", a=2, j=2),
-                in0=prod[g][:].rearrange("p (a j f) -> p a j f", a=2, j=2),
-                in1=centroid_jqs[:, :, q0 : q0 + IMG, :].rearrange("p j (a b) s -> p a j (b s)", a=2, b=2),
+                in0=mm[g][:].rearrange("p (a j f) -> p a j f", a=2, j=2),
+                in1=csb4[:, :, IMG * h : IMG * (h + 1), :].rearrange("p j (a b) s -> p a j (b s)", a=2, b=2),
                 op=ALU.subtract,
             )
 
-        def transpose_diff(g):
-            if g < SUPPORT_STEPS or g >= STEPS:
+        def dtr(g):
+            if g < HALF or g >= NSTEP:
                 return
-            diff_t[g] = psum.tile([P, 4 * P], F32, name="diff_t", tag="small", bufs=2)
+            dt[g] = psum.tile([P, 512], F32, name="dt", tag="aux", bufs=2)
             for b in range(4):
-                nc.tensor.transpose(diff_t[g][:, b * P : (b + 1) * P], diff[g][:, b * P : (b + 1) * P], ident[:])
+                nc.tensor.transpose(dt[g][:, b * P : (b + 1) * P], diff[g][:, b * P : (b + 1) * P], ident[:])
 
-        def square_and_sum(g):
-            if g < SUPPORT_STEPS or g >= STEPS:
+        def sq(g):
+            if g < HALF or g >= NSTEP:
                 return
+            h = g - HALF
             for a in range(2):
-                pair = 2 * (g - SUPPORT_STEPS) + a
-                squares = work.tile([P, D], F32, name="squares", tag="squares")
+                junk = work.tile([P, 256], F32, name="junk", tag="junk")
                 nc.scalar.activation(
-                    out=squares[:],
-                    in_=diff_t[g][:, a * D : (a + 1) * D],
+                    out=junk[:],
+                    in_=dt[g][:, a * 256 : (a + 1) * 256],
                     func=ACT.Square,
-                    accum_out=l2_cols[:, pair : pair + 1],
+                    accum_out=l2col[:, 2 * h + a : 2 * h + a + 1],
                 )
 
-        ctx.enter_context(tc.manual_schedule())
+        if PIN:
+            ctx.enter_context(tc.manual_schedule())
+
         for g in range(LOOKAHEAD):
             load(g)
-        for k in range(STEPS + 6):
+        for k in range(NSTEP + 6):
             load(k + LOOKAHEAD)
-            group_weights(k - 1)
-            subtract(k - 3)
-            quantise_images(k - 1)
-            quantise_weights_sq(k - 1)
-            if k == SUPPORT_STEPS + 1:
-                quantise_weights_qs(0)
-            if k in (SUPPORT_STEPS + 4, SUPPORT_STEPS + 8, SUPPORT_STEPS + 12):
-                quantise_weights_qs((k - SUPPORT_STEPS) // 4)
-            square_and_sum(k - 5)
-            park_centroid(k - 3)
-            transpose_diff(k - 4)
+            copies_w(k - 1)
+            sub(k - 3)
+            quant_x(k - 1)
+            quant_wa(k - 1)
+            if k == HALF + 1:
+                quant_wb(0)
+            if k in (HALF + 4, HALF + 8, HALF + 12):
+                quant_wb((k - HALF) // 4)
+            sq(k - 5)
+            ccopy(k - 3)
+            dtr(k - 4)
             if k == 0:
-                transpose_image(0, 0)
-            transpose_weights(k)
+                transp_x(0, 0)
+            transp_w(k)
             for i in range(1 if k == 0 else 0, IMG):
-                transpose_image(k, i)
-            multiply(k - 2)
-            group_images(k)
+                transp_x(k, i)
+            mx(k - 2)
+            copies_x(k)
 
-        l2_rows = psum.tile([P, P], F32, name="l2_rows", tag="small", bufs=2)
-        nc.tensor.transpose(l2_rows[:], l2_cols[:], ident[:])
-        logits = keep.tile([P, 2, NS], F32)
-        nc.vector.tensor_scalar_mul(logits[:].rearrange("p a s -> p (a s)"), l2_rows[:], factor[:, 0:1])
-        top = keep.tile([P, 2], F32)
-        nc.vector.tensor_reduce(out=top[:], in_=logits[:], axis=AX.X, op=ALU.max)
-        shifted = keep.tile([P, 2, NS], F32)
+        l2t = psum.tile([P, P], F32, name="l2t", tag="aux", bufs=2)
+        nc.tensor.transpose(l2t[:], l2col[:], ident[:])
+        lg = const.tile([P, 2, NS], F32)
+        nc.vector.tensor_scalar_mul(lg[:].rearrange("p a s -> p (a s)"), l2t[:], a_sb[:, 0:1])
+        top = const.tile([P, 2], F32)
+        nc.vector.tensor_reduce(out=top[:], in_=lg[:], axis=AX.X, op=ALU.max)
+        z = const.tile([P, 2, NS], F32)
         nc.vector.tensor_tensor(
-            out=shifted[:], in0=logits[:], in1=top[:].unsqueeze(2).to_broadcast([P, 2, NS]), op=ALU.subtract
+            out=z[:], in0=lg[:], in1=top[:].unsqueeze(2).to_broadcast([P, 2, NS]), op=ALU.subtract
         )
-        exps = keep.tile([P, 2, NS], F32)
-        total = keep.tile([P, 2], F32)
+        ez = const.tile([P, 2, NS], F32)
+        tot = const.tile([P, 2], F32)
         for a in range(2):
-            nc.scalar.activation(out=exps[:, a, :], in_=shifted[:, a, :], func=ACT.Exp, accum_out=total[:, a : a + 1])
-        log_total = keep.tile([P, 2], F32)
-        nc.scalar.activation(out=log_total[:], in_=total[:], func=ACT.Ln)
-        result = keep.tile([P, 2, NS], F32)
+            nc.scalar.activation(out=ez[:, a, :], in_=z[:, a, :], func=ACT.Exp, accum_out=tot[:, a : a + 1])
+        ltot = const.tile([P, 2], F32)
+        nc.scalar.activation(out=ltot[:], in_=tot[:], func=ACT.Ln)
+        res = const.tile([P, 2, NS], F32)
         nc.vector.tensor_tensor(
-            out=result[:], in0=shifted[:], in1=log_total[:].unsqueeze(2).to_broadcast([P, 2, NS]), op=ALU.subtract
+            out=res[:], in0=z[:], in1=ltot[:].unsqueeze(2).to_broadcast([P, 2, NS]), op=ALU.subtract
         )
         nc.sync.dma_start(
-            out=out.rearrange("(u a) s -> u (a s)", a=2), in_=result[0 : NQ // 2].rearrange("p a s -> p (a s)")
+            out=out.rearrange("(u a) s -> u (a s)", a=2), in_=res[0:32].rearrange("p a s -> p (a s)")
         )

@@ -23,7 +23,7 @@ FLOPS = 2 * 2 * NS * NQ * D * M
 IMG = 4
 NSTEP = (NS + NQ) // IMG
 HALF = NS // IMG
-LOOKAHEAD = 4
+LOOKAHEAD = 5
 PIN = True
 WIDTHS = (128, 128, 128, 128, 128, 128, 128, 64)
 
@@ -51,7 +51,7 @@ def tile_proto_t_kernel(tc, feature_map, weight2, scale, out):
         csb = const.tile([P, 2 * NQ * NS], F32)
         csb4 = csb[:].rearrange("p (j q s) -> p j q s", j=2, q=NQ, s=NS)
         gb = const.tile([P, NQ * NS * 4], BF16, align_bytes=64)
-        gb4 = gb[:].bitcast(F32).rearrange("p (q s u) -> p q s u", q=NQ, s=NS, u=2)
+        gb5 = gb[:].bitcast(F32).rearrange("p (b r s u) -> p b r s u", b=NQ // 2, r=2, s=NS, u=2)
         wbc = const.tile([P, NQ * NS + 64], U32, align_bytes=64)
         wbs = const.tile([P, NQ * NS + 64], U8, align_bytes=64)
         wac = const.tile([P, NQ * NS + 64], U32, align_bytes=64)
@@ -59,7 +59,6 @@ def tile_proto_t_kernel(tc, feature_map, weight2, scale, out):
         for pad in (wbc, wbs, wac, was):
             nc.vector.memset(pad[:, NQ * NS : NQ * NS + 64].bitcast(I32), 0)
 
-        wrows = weight2.rearrange("s q m -> (s q) m").rearrange("(t p) m -> p t m", p=P)
 
         xs = {}
         ws = {}
@@ -88,7 +87,8 @@ def tile_proto_t_kernel(tc, feature_map, weight2, scale, out):
             if g < HALF:
                 ws[g] = wpool.tile([P, 2 * M], BF16, name="ws", tag="ws")
                 nc.sync.dma_start(
-                    out=ws[g][:].rearrange("p (t m) -> p t m", t=2), in_=wrows[:, 2 * g : 2 * g + 2, :]
+                    out=ws[g][:],
+                    in_=weight2[IMG * g : IMG * (g + 1)].rearrange("s q m -> (s q) m").rearrange("(p r) m -> p (r m)", r=2),
                 )
             if g == 0:
                 for i in range(1, IMG):
@@ -137,12 +137,12 @@ def tile_proto_t_kernel(tc, feature_map, weight2, scale, out):
                 return
             ga[g] = work.tile([P, 1024], BF16, name="ga", tag="ga", align_bytes=64)
             nc.vector.tensor_copy(
-                out=ga[g][:].bitcast(F32).rearrange("p (c u) -> p c u", u=2),
-                in_=wt[g][:].rearrange("p u c -> p c u"),
+                out=ga[g][:].bitcast(F32).rearrange("p (c r u) -> p c r u", r=2, u=2),
+                in_=wt[g][:].rearrange("p u (r c) -> p c r u", r=2),
             )
             nc.vector.tensor_copy(
-                out=gb4[:, :, IMG * g : IMG * (g + 1), :],
-                in_=wt[g][:].rearrange("p u (s q) -> p q s u", s=IMG, q=NQ),
+                out=gb5[:, :, :, IMG * g : IMG * (g + 1), :],
+                in_=wt[g][:].rearrange("p u (r s b) -> p b r s u", r=2, s=IMG),
             )
 
         def copies_x(g):

from contextlib import ExitStack

import concourse.mybir as mybir
from concourse.masks import make_identity

F32 = mybir.dt.float32
BF16 = mybir.dt.bfloat16
U32 = mybir.dt.uint32
U8 = mybir.dt.uint8
I32 = mybir.dt.int32
FP8X4 = mybir.dt.float8_e4m3fn_x4
ACT = mybir.ActivationFunctionType
ALU = mybir.AluOpType
AX = mybir.AxisListType

P = 128
NS = 64
NQ = 64
D = 256
M = 512
FLOPS = 2 * 2 * NS * NQ * D * M

IMG = 4
NSTEP = (NS + NQ) // IMG
HALF = NS // IMG
LOOKAHEAD = 5
PIN = True
WIDTHS = (128, 128, 128, 128, 128, 128, 128, 64)


def tile_proto_t_kernel(tc, feature_map, weight2, scale, out):
    nc = tc.nc
    with ExitStack() as ctx:
        const = ctx.enter_context(tc.tile_pool(name="const", bufs=1))
        xpool = ctx.enter_context(tc.tile_pool(name="xpool", bufs=LOOKAHEAD + 1))
        wpool = ctx.enter_context(tc.tile_pool(name="wpool", bufs=LOOKAHEAD + 1))
        work = ctx.enter_context(tc.tile_pool(name="work", bufs=3))
        psum = ctx.enter_context(tc.psum_pool(name="psum", bufs=2))

        ident = const.tile([P, P], F32)
        make_identity(nc, ident[:])
        sc_bf = const.tile([P, 1], BF16)
        nc.scalar.dma_start(out=sc_bf[:], in_=scale.partition_broadcast(P))
        a_sb = const.tile([P, 1], F32)
        nc.vector.tensor_scalar_mul(a_sb[:], sc_bf[:], -1.0 / (800.0 * M * M))
        l2col = const.tile([P, P], F32)
        nc.vector.memset(l2col[:], 0.0)
        warm = const.tile([P, 1], F32)
        nc.scalar.activation(out=warm[:], in_=l2col[:, 0:1], func=ACT.Exp)

        csb = const.tile([P, 2 * NQ * NS], F32)
        csb4 = csb[:].rearrange("p (j q s) -> p j q s", j=2, q=NQ, s=NS)
        gb = const.tile([P, NQ * NS * 4], BF16, align_bytes=64)
        gb5 = gb[:].bitcast(F32).rearrange("p (b r s u) -> p b r s u", b=NQ // 2, r=2, s=NS, u=2)
        wbc = const.tile([P, NQ * NS + 64], U32, align_bytes=64)
        wbs = const.tile([P, NQ * NS + 64], U8, align_bytes=64)
        wac = const.tile([P, NQ * NS + 64], U32, align_bytes=64)
        was = const.tile([P, NQ * NS + 64], U8, align_bytes=64)
        for pad in (wbc, wbs, wac, was):
            nc.vector.memset(pad[:, NQ * NS : NQ * NS + 64].bitcast(I32), 0)


        xs = {}
        ws = {}
        xt = {}
        wt = {}
        gx = {}
        ga = {}
        xc = {}
        xsc = {}
        mm = {}
        diff = {}
        dt = {}

        def load(g):
            if g >= NSTEP:
                return
            xs[g] = xpool.tile([P, IMG * 1024], BF16, name="xs", tag="xs")
            dst = xs[g][:].rearrange("p (b f) -> p b f", b=IMG)
            src = (
                feature_map[IMG * g : IMG * (g + 1)]
                .rearrange("i d m -> (i d) m")
                .rearrange("(p b r) m -> p b (r m)", b=IMG, r=2)
            )
            if g == 0:
                nc.sync.dma_start(out=dst[:, 0, :], in_=src[:, 0, :])
            if g < HALF:
                ws[g] = wpool.tile([P, 2 * M], BF16, name="ws", tag="ws")
                nc.sync.dma_start(
                    out=ws[g][:],
                    in_=weight2[IMG * g : IMG * (g + 1)].rearrange("s q m -> (s q) m").rearrange("(p r) m -> p (r m)", r=2),
                )
            if g == 0:
                for i in range(1, IMG):
                    nc.sync.dma_start(out=dst[:, i, :], in_=src[:, i, :])
            else:
                nc.sync.dma_start(
                    out=xs[g][:],
                    in_=feature_map[IMG * g : IMG * (g + 1)]
                    .rearrange("i d m -> (i d) m")
                    .rearrange("(p r) m -> p (r m)", r=2 * IMG),
                )

        def transp_w(g):
            if g >= HALF:
                return
            wt[g] = psum.tile([P, 2, 256], F32, name="wt", tag="aux", bufs=2)
            ww = ws[g][:].bitcast(F32)
            for t in range(2):
                for u in range(2):
                    nc.tensor.transpose(
                        wt[g][:, u, t * P : (t + 1) * P], ww[:, t * 256 + u * P : t * 256 + (u + 1) * P], ident[:]
                    )

        def transp_x(g, i):
            if g >= NSTEP:
                return
            xw = xs[g][:].bitcast(F32)
            xt[g, i] = psum.tile([P, 2, IMG, 2, 32], F32, name="xt", tag="xt", bufs=4)
            for j in range(2):
                for u in range(2):
                    c0 = i * 512 + j * 256 + u * P
                    nc.tensor.transpose(
                        xt[g, i][:, u, :, j, :], xw[:, c0 : c0 + P], ident[:].rearrange("p (i c) -> p i c", i=IMG)
                    )

        def copy_x(g, i, on_vector):
            dst = gx[g][:].bitcast(F32).rearrange("p (i b c u) -> p i b c u", i=IMG, b=IMG, c=64, u=2)[:, :, i, :, :]
            src = xt[g, i][:].rearrange("p u i r c -> p i (r c) u")
            if on_vector:
                nc.vector.tensor_copy(out=dst, in_=src)
            else:
                nc.scalar.copy(out=dst, in_=src)

        def copies_w(g):
            if g < 0 or g >= HALF:
                return
            ga[g] = work.tile([P, 1024], BF16, name="ga", tag="ga", align_bytes=64)
            nc.vector.tensor_copy(
                out=ga[g][:].bitcast(F32).rearrange("p (c r u) -> p c r u", r=2, u=2),
                in_=wt[g][:].rearrange("p u (r c) -> p c r u", r=2),
            )
            nc.vector.tensor_copy(
                out=gb5[:, :, :, IMG * g : IMG * (g + 1), :],
                in_=wt[g][:].rearrange("p u (r s b) -> p b r s u", r=2, s=IMG),
            )

        def copies_x(g):
            if g >= NSTEP:
                return
            gx[g] = work.tile([P, IMG * 1024], BF16, name="gx", tag="gx", align_bytes=64)
            for i in range(IMG):
                if g == NSTEP - 1:
                    copy_x(g, i, i % 2 == 1)
                else:
                    copy_x(g, i, g >= HALF and i == IMG - 1)

        def quant_wa(g):
            if g < 0 or g >= HALF:
                return
            nc.vector.quantize_mx(
                out=wac[:, 256 * g : 256 * (g + 1)].bitcast(FP8X4), scales=was[:, 256 * g : 256 * (g + 1)], in_=ga[g][:]
            )

        def quant_wb(k):
            nc.vector.quantize_mx(
                out=wbc[:, k * 1024 : (k + 1) * 1024].bitcast(FP8X4),
                scales=wbs[:, k * 1024 : (k + 1) * 1024],
                in_=gb[:, k * 4096 : (k + 1) * 4096],
            )

        def quant_x(g):
            if g < 0 or g >= NSTEP:
                return
            xc[g] = work.tile([P, IMG * 256], U32, name="xc", tag="xc", align_bytes=64)
            xsc[g] = work.tile([P, IMG * 256], U8, name="xsc", tag="xsc", align_bytes=64)
            pieces = 1
            wid = IMG * 256 // pieces
            for h in range(pieces):
                nc.vector.quantize_mx(
                    out=xc[g][:, h * wid : (h + 1) * wid].bitcast(FP8X4),
                    scales=xsc[g][:, h * wid : (h + 1) * wid],
                    in_=gx[g][:, 4 * h * wid : 4 * (h + 1) * wid],
                )

        def mx(g):
            if g < 0 or g >= NSTEP:
                return
            mm[g] = psum.tile([P, 512], F32, name="mm", tag="mm", bufs=2)
            for slot in range(8):
                if g < HALF:
                    j, i = slot // IMG, slot % IMG
                    codes, planes = wac, was
                else:
                    i, j = (slot // 4) * 2 + slot % 2, (slot // 2) % 2
                    codes, planes = wbc, wbs
                c0 = i * 256 + j * P
                w0 = (IMG * (g % HALF) + i) * 64
                n = WIDTHS[slot]
                nc.tensor.matmul_mx(
                    out=mm[g][:, slot * 64 : slot * 64 + n],
                    lhsT=xc[g][:, c0 : c0 + P].bitcast(FP8X4),
                    lhsT_scale=xsc[g][:, c0 : c0 + P],
                    rhs=codes[:, w0 : w0 + n].bitcast(FP8X4),
                    rhs_scale=planes[:, w0 : w0 + n],
                    start=True,
                    stop=True,
                )

        def ccopy(g):
            if g < 0 or g >= HALF:
                return
            nc.scalar.copy(
                out=csb4[:, :, :, IMG * g : IMG * (g + 1)],
                in_=mm[g][:].rearrange("p (j i q) -> p j q i", j=2, i=IMG, q=NQ),
            )

        def sub(g):
            if g < HALF or g >= NSTEP:
                return
            h = g - HALF
            diff[g] = work.tile([P, 512], F32, name="diff", tag="diff")
            nc.vector.tensor_tensor(
                out=diff[g][:].rearrange("p (a j f) -> p a j f", a=2, j=2),
                in0=mm[g][:].rearrange("p (a j f) -> p a j f", a=2, j=2),
                in1=csb4[:, :, IMG * h : IMG * (h + 1), :].rearrange("p j (a b) s -> p a j (b s)", a=2, b=2),
                op=ALU.subtract,
            )

        def dtr(g):
            if g < HALF or g >= NSTEP:
                return
            dt[g] = psum.tile([P, 512], F32, name="dt", tag="aux", bufs=2)
            for b in range(4):
                nc.tensor.transpose(dt[g][:, b * P : (b + 1) * P], diff[g][:, b * P : (b + 1) * P], ident[:])

        def sq(g):
            if g < HALF or g >= NSTEP:
                return
            h = g - HALF
            for a in range(2):
                junk = work.tile([P, 256], F32, name="junk", tag="junk")
                nc.scalar.activation(
                    out=junk[:],
                    in_=dt[g][:, a * 256 : (a + 1) * 256],
                    func=ACT.Square,
                    accum_out=l2col[:, 2 * h + a : 2 * h + a + 1],
                )

        if PIN:
            ctx.enter_context(tc.manual_schedule())

        for g in range(LOOKAHEAD):
            load(g)
        for k in range(NSTEP + 6):
            load(k + LOOKAHEAD)
            copies_w(k - 1)
            sub(k - 3)
            quant_x(k - 1)
            quant_wa(k - 1)
            if k == HALF + 1:
                quant_wb(0)
            if k in (HALF + 4, HALF + 8, HALF + 12):
                quant_wb((k - HALF) // 4)
            sq(k - 5)
            ccopy(k - 3)
            dtr(k - 4)
            if k == 0:
                transp_x(0, 0)
            transp_w(k)
            for i in range(1 if k == 0 else 0, IMG):
                transp_x(k, i)
            mx(k - 2)
            copies_x(k)

        l2t = psum.tile([P, P], F32, name="l2t", tag="aux", bufs=2)
        nc.tensor.transpose(l2t[:], l2col[:], ident[:])
        lg = const.tile([P, 2, NS], F32)
        nc.vector.tensor_scalar_mul(lg[:].rearrange("p a s -> p (a s)"), l2t[:], a_sb[:, 0:1])
        top = const.tile([P, 2], F32)
        nc.vector.tensor_reduce(out=top[:], in_=lg[:], axis=AX.X, op=ALU.max)
        z = const.tile([P, 2, NS], F32)
        nc.vector.tensor_tensor(
            out=z[:], in0=lg[:], in1=top[:].unsqueeze(2).to_broadcast([P, 2, NS]), op=ALU.subtract
        )
        ez = const.tile([P, 2, NS], F32)
        tot = const.tile([P, 2], F32)
        for a in range(2):
            nc.scalar.activation(out=ez[:, a, :], in_=z[:, a, :], func=ACT.Exp, accum_out=tot[:, a : a + 1])
        ltot = const.tile([P, 2], F32)
        nc.scalar.activation(out=ltot[:], in_=tot[:], func=ACT.Ln)
        res = const.tile([P, 2, NS], F32)
        nc.vector.tensor_tensor(
            out=res[:], in0=z[:], in1=ltot[:].unsqueeze(2).to_broadcast([P, 2, NS]), op=ALU.subtract
        )
        nc.sync.dma_start(
            out=out.rearrange("(u a) s -> u (a s)", a=2), in_=res[0:32].rearrange("p a s -> p (a s)")
        )
